import numpy as np
import ml_dtypes


def mxq(x, axis, fmt="e4m3"):
    dtype, down = {"e4m3": (ml_dtypes.float8_e4m3fn, 7), "e5m2": (ml_dtypes.float8_e5m2, 14)}[fmt]
    v = np.moveaxis(np.asarray(x, np.float32).astype(ml_dtypes.bfloat16).astype(np.float64), axis, -1)
    blocks = v.reshape(v.shape[:-1] + (-1, 32))
    amax = np.abs(blocks).max(-1, keepdims=True)
    byte = np.maximum(np.where(amax > 0, np.frexp(amax)[1] - 1 + 127, 0) - down, 1)
    scale = np.exp2(byte - 127.0)
    codes = (blocks / scale).astype(np.float32).astype(dtype).astype(np.float64)
    return np.moveaxis((codes * scale).reshape(v.shape), -1, axis)


WIDE = False


def mx_kscale(k):
    if not WIDE:
        return np.ones(k)
    levels = np.array([20, -20, 10, -10, 0])
    a = np.random.permutation(np.resize(levels, k // 512 * 4)).reshape(k // 512, 4)
    idx = np.arange(k)
    return np.exp2(a[idx // 512, idx % 128 // 32])


BF16 = ml_dtypes.bfloat16


def bf(x):
    return np.asarray(x, np.float32).astype(BF16)


def f64(x):
    return np.asarray(x).astype(np.float64)


BLOCK = 128
B, S, K, N = 2, 256, 7168, 512


def setup_inputs():
    u = mx_kscale(N)
    x = np.random.standard_normal((B, S, K))
    weight = np.random.standard_normal((N, K)) * 0.02 / u[:, None]
    weight_scale = np.random.uniform(0.5, 1.5, (N // BLOCK, K // BLOCK))
    g = np.random.standard_normal((B, S, N)) * np.exp2(np.random.randint(-12, 1, (B, S, 1))) * 16.0 * u
    return {"x": bf(x), "weight": bf(weight), "weight_scale": bf(weight_scale), "grad_out": bf(g)}


def w_dequant(weight, weight_scale):
    weight = f64(weight)
    n, k = weight.shape
    ws = np.repeat(np.repeat(f64(weight_scale), BLOCK, axis=0)[:n], BLOCK, axis=1)[:, :k]
    return weight * ws


def reference(x, weight_scale, weight, grad_out):
    g = f64(grad_out)
    lead = g.shape[:-1]
    w_deq = w_dequant(weight, weight_scale)
    n, k = w_deq.shape
    gx = mxq(g.reshape(-1, n), 1, "e5m2") @ mxq(w_deq, 0, "e4m3")
    return gx.reshape(*lead, k)

@@ -1,0 +1,147 @@
+from contextlib import ExitStack
+
+import concourse.mybir as mybir
+from concourse.masks import make_identity
+
+F32 = mybir.dt.float32
+BF16 = mybir.dt.bfloat16
+U32 = mybir.dt.uint32
+U8 = mybir.dt.uint8
+E4M3X4 = mybir.dt.float8_e4m3fn_x4
+E5M2X4 = mybir.dt.float8_e5m2_x4
+MULT = mybir.AluOpType.mult
+
+P = 128
+PACK = 4
+TOK = 512
+N = 512
+K = 7168
+BLOCK = 128
+SUB = 512
+N_SUB = K // SUB
+M_TILES = TOK // P
+
+LOAD_WIDTHS = (512, 1024, 2048, 3584)
+STORE_SUBS = (2, 3, 3, 3, 3)
+STAGE_BUFS = 16
+
+FLOPS = 2 * TOK * N * K
+BYTES = N * K * 2 + (N // BLOCK) * (K // BLOCK) * 2 + TOK * N * 2 + TOK * K * 4
+
+
+def tile_lineardeepseekv3_kernel(tc, x, weight, weight_scale, grad_out, out):
+    nc = tc.nc
+    g_rows = grad_out.flatten_outer_dims()
+    out_v = out.flatten_outer_dims().rearrange("(p m) k -> p m k", m=M_TILES)
+    w_v = weight.rearrange("(p j) k -> p j k", j=PACK)
+
+    with ExitStack() as ctx:
+        keep = ctx.enter_context(tc.tile_pool(name="keep", bufs=1))
+        grp = ctx.enter_context(tc.tile_pool(name="grp", bufs=3))
+        stage = ctx.enter_context(tc.tile_pool(name="stage", bufs=STAGE_BUFS))
+        psum = ctx.enter_context(tc.psum_pool(name="psum", bufs=8))
+
+        wsz = keep.tile([P, 64], BF16)
+        nc.vector.memset(wsz[:], 0.0)
+        g_sb = keep.tile([P, M_TILES * N], BF16)
+        nc.sync.dma_start(out=g_sb[:], in_=g_rows.rearrange("(p m) n -> p (m n)", m=M_TILES))
+        nc.sync.dma_start(out=wsz[0:P:32, 0 : K // BLOCK], in_=weight_scale)
+
+        raws = []
+        c0 = 0
+        for i, width in enumerate(LOAD_WIDTHS):
+            raw = keep.tile([P, PACK, width], BF16, name="raw%d" % i)
+            nc.sync.dma_start(out=raw[:], in_=w_v[:, :, c0 : c0 + width])
+            for s in range(width // SUB):
+                raws.append((raw, s * SUB))
+            c0 += width
+
+        sel = keep.tile([P, P], BF16)
+        nc.vector.memset(sel[:], 0.0)
+        for r in range(4):
+            nc.vector.memset(sel[32 * r : 32 * r + 32, 32 * r : 32 * r + 32], 1.0)
+        ident = keep.tile([P, P], F32)
+        make_identity(nc, ident[:])
+
+        ws_ps = psum.tile([P, 64], F32, tag="bank")
+        nc.tensor.matmul(out=ws_ps[:], lhsT=sel[:], rhs=wsz[:], start=True, stop=True)
+        ws_f = keep.tile([P, 64], F32)
+        nc.vector.tensor_copy(out=ws_f[:], in_=ws_ps[:])
+
+        g_w = g_sb[:].bitcast(F32).rearrange("p (m w u) -> p m w u", m=M_TILES, u=2)
+        gg = keep.tile([P, M_TILES * P * PACK], BF16, align_bytes=64)
+        gg_w = gg[:].bitcast(F32).rearrange("p (m r u) -> p m r u", m=M_TILES, u=2)
+        for h in range(2):
+            xt = psum.tile([P, 2, 2, P], F32, tag="bank")
+            for mm in range(2):
+                for u in range(2):
+                    nc.tensor.transpose(xt[:, mm, u, :], g_w[:, 2 * h + mm, :, u], ident[:])
+            src = xt[:].rearrange("p m u r -> p m r u")
+            if h == 0:
+                nc.vector.tensor_copy(out=gg_w[:, 0:2, :, :], in_=src)
+            else:
+                nc.scalar.copy(out=gg_w[:, 2:4, :, :], in_=src)
+        g_codes = keep.tile([P, TOK], U32, align_bytes=64)
+        g_scales = keep.tile([P, TOK], U8, align_bytes=64)
+        nc.vector.quantize_mx(out=g_codes[:].bitcast(E5M2X4), scales=g_scales[:], in_=gg[:])
+
+        w_codes = keep.tile([P, K], U32, align_bytes=64)
+        w_scales = keep.tile([P, K], U8, align_bytes=64)
+        grouped = {}
+
+        def prep(s):
+            raw, off = raws[s]
+            gt = grp.tile([P, SUB, PACK], BF16, name="gt", align_bytes=64)
+            grouped[s] = gt
+            for b in range(SUB // BLOCK):
+                blk = s * (SUB // BLOCK) + b
+                nc.vector.tensor_scalar(
+                    out=gt[:, b * BLOCK : (b + 1) * BLOCK, :].rearrange("p (c i) t -> p c t i", i=4),
+                    in0=raw[:, :, off + b * BLOCK : off + (b + 1) * BLOCK].rearrange("p t (c i) -> p c t i", i=4),
+                    scalar1=ws_f[:, blk : blk + 1],
+                    scalar2=None,
+                    op0=MULT,
+                )
+
+        def quant(s):
+            cols = slice(s * SUB, (s + 1) * SUB)
+            nc.vector.quantize_mx(
+                out=w_codes[:, cols].bitcast(E4M3X4),
+                scales=w_scales[:, cols],
+                in_=grouped[s][:].rearrange("p w t -> p (w t)"),
+            )
+
+        group_of = []
+        for gi, n_sub in enumerate(STORE_SUBS):
+            for j in range(n_sub):
+                group_of.append((gi, j, n_sub))
+        stages = {}
+
+        def multiply(s):
+            gi, j, n_sub = group_of[s]
+            cols = slice(s * SUB, (s + 1) * SUB)
+            for m in range(M_TILES):
+                if j == 0:
+                    stages[m] = stage.tile([P, n_sub * SUB], F32, name="st%d" % m, tag="st")
+                acc = psum.tile([P, SUB], F32, tag="bank")
+                toks = slice(m * P, (m + 1) * P)
+                nc.tensor.matmul_mx(
+                    out=acc[:],
+                    lhsT=g_codes[:, toks].bitcast(E5M2X4),
+                    lhsT_scale=g_scales[:, toks],
+                    rhs=w_codes[:, cols].bitcast(E4M3X4),
+                    rhs_scale=w_scales[:, cols],
+                    start=True,
+                    stop=True,
+                )
+                nc.scalar.copy(out=stages[m][:, j * SUB : (j + 1) * SUB], in_=acc[:])
+                if j == n_sub - 1:
+                    first = (s + 1 - n_sub) * SUB
+                    nc.sync.dma_start(out=out_v[:, m, first : (s + 1) * SUB], in_=stages[m][:])
+
+        prep(0)
+        for s in range(N_SUB):
+            if s + 1 < N_SUB:
+                prep(s + 1)
+            quant(s)
+            multiply(s)

@@ -20,10 +20,11 @@ BLOCK = 128
 SUB = 512
 N_SUB = K // SUB
 M_TILES = TOK // P
+BLOCKS_PER_SUB = SUB // BLOCK
 
 LOAD_WIDTHS = (512, 1024, 2048, 3584)
-STORE_SUBS = (2, 3, 3, 3, 3)
-STAGE_BUFS = 16
+STORE_ENDS = ((3, 8, 14), (4, 9, 14), (5, 10, 14), (6, 11, 14))
+VECTOR_BANKS = ((11, 3), (12, 2), (12, 3), (13, 2), (13, 3))
 
 FLOPS = 2 * TOK * N * K
 BYTES = N * K * 2 + (N // BLOCK) * (K // BLOCK) * 2 + TOK * N * 2 + TOK * K * 4
@@ -38,20 +39,22 @@ def tile_lineardeepseekv3_kernel(tc, x, weight, weight_scale, grad_out, out):
     with ExitStack() as ctx:
         keep = ctx.enter_context(tc.tile_pool(name="keep", bufs=1))
         grp = ctx.enter_context(tc.tile_pool(name="grp", bufs=3))
-        stage = ctx.enter_context(tc.tile_pool(name="stage", bufs=STAGE_BUFS))
+        cod = ctx.enter_context(tc.tile_pool(name="cod", bufs=6))
         psum = ctx.enter_context(tc.psum_pool(name="psum", bufs=8))
+        ctx.enter_context(tc.manual_schedule())
 
         wsz = keep.tile([P, 64], BF16)
         nc.vector.memset(wsz[:], 0.0)
         g_sb = keep.tile([P, M_TILES * N], BF16)
         nc.sync.dma_start(out=g_sb[:], in_=g_rows.rearrange("(p m) n -> p (m n)", m=M_TILES))
         nc.sync.dma_start(out=wsz[0:P:32, 0 : K // BLOCK], in_=weight_scale)
-
         raws = []
+        chunk_starts = []
         c0 = 0
         for i, width in enumerate(LOAD_WIDTHS):
             raw = keep.tile([P, PACK, width], BF16, name="raw%d" % i)
             nc.sync.dma_start(out=raw[:], in_=w_v[:, :, c0 : c0 + width])
+            chunk_starts.append(c0 // SUB)
             for s in range(width // SUB):
                 raws.append((raw, s * SUB))
             c0 += width
@@ -62,7 +65,6 @@ def tile_lineardeepseekv3_kernel(tc, x, weight, weight_scale, grad_out, out):
             nc.vector.memset(sel[32 * r : 32 * r + 32, 32 * r : 32 * r + 32], 1.0)
         ident = keep.tile([P, P], F32)
         make_identity(nc, ident[:])
-
         ws_ps = psum.tile([P, 64], F32, tag="bank")
         nc.tensor.matmul(out=ws_ps[:], lhsT=sel[:], rhs=wsz[:], start=True, stop=True)
         ws_f = keep.tile([P, 64], F32)
@@ -76,72 +78,86 @@ def tile_lineardeepseekv3_kernel(tc, x, weight, weight_scale, grad_out, out):
             for mm in range(2):
                 for u in range(2):
                     nc.tensor.transpose(xt[:, mm, u, :], g_w[:, 2 * h + mm, :, u], ident[:])
-            src = xt[:].rearrange("p m u r -> p m r u")
-            if h == 0:
-                nc.vector.tensor_copy(out=gg_w[:, 0:2, :, :], in_=src)
-            else:
-                nc.scalar.copy(out=gg_w[:, 2:4, :, :], in_=src)
-        g_codes = keep.tile([P, TOK], U32, align_bytes=64)
-        g_scales = keep.tile([P, TOK], U8, align_bytes=64)
-        nc.vector.quantize_mx(out=g_codes[:].bitcast(E5M2X4), scales=g_scales[:], in_=gg[:])
+            nc.scalar.copy(out=gg_w[:, 2 * h : 2 * h + 2, :, :], in_=xt[:].rearrange("p m u r -> p m r u"))
 
-        w_codes = keep.tile([P, K], U32, align_bytes=64)
-        w_scales = keep.tile([P, K], U8, align_bytes=64)
         grouped = {}
+        codes = {}
 
-        def prep(s):
+        def regroup(s, blocks):
             raw, off = raws[s]
-            gt = grp.tile([P, SUB, PACK], BF16, name="gt", align_bytes=64)
-            grouped[s] = gt
-            for b in range(SUB // BLOCK):
-                blk = s * (SUB // BLOCK) + b
+            if s not in grouped:
+                grouped[s] = grp.tile([P, SUB, PACK], BF16, name="gt", align_bytes=64)
+            gt = grouped[s]
+            for b in blocks:
                 nc.vector.tensor_scalar(
                     out=gt[:, b * BLOCK : (b + 1) * BLOCK, :].rearrange("p (c i) t -> p c t i", i=4),
                     in0=raw[:, :, off + b * BLOCK : off + (b + 1) * BLOCK].rearrange("p t (c i) -> p c t i", i=4),
-                    scalar1=ws_f[:, blk : blk + 1],
+                    scalar1=ws_f[:, s * BLOCKS_PER_SUB + b : s * BLOCKS_PER_SUB + b + 1],
                     scalar2=None,
                     op0=MULT,
                 )
 
-        def quant(s):
-            cols = slice(s * SUB, (s + 1) * SUB)
+        def quantise(s):
+            wc = cod.tile([P, SUB], U32, name="wc", align_bytes=64)
+            wp = cod.tile([P, SUB], U8, name="wp", align_bytes=64)
+            codes[s] = (wc, wp)
             nc.vector.quantize_mx(
-                out=w_codes[:, cols].bitcast(E4M3X4),
-                scales=w_scales[:, cols],
-                in_=grouped[s][:].rearrange("p w t -> p (w t)"),
+                out=wc[:].bitcast(E4M3X4), scales=wp[:], in_=grouped[s][:].rearrange("p w t -> p (w t)")
             )
 
-        group_of = []
-        for gi, n_sub in enumerate(STORE_SUBS):
-            for j in range(n_sub):
-                group_of.append((gi, j, n_sub))
+        regroup(0, range(BLOCKS_PER_SUB))
+        g_codes = keep.tile([P, TOK], U32, align_bytes=64)
+        g_scales = keep.tile([P, TOK], U8, align_bytes=64)
+        nc.vector.quantize_mx(out=g_codes[:].bitcast(E5M2X4), scales=g_scales[:], in_=gg[:])
+
         stages = {}
+        banks = {}
 
-        def multiply(s):
-            gi, j, n_sub = group_of[s]
-            cols = slice(s * SUB, (s + 1) * SUB)
-            for m in range(M_TILES):
-                if j == 0:
-                    stages[m] = stage.tile([P, n_sub * SUB], F32, name="st%d" % m, tag="st")
-                acc = psum.tile([P, SUB], F32, tag="bank")
-                toks = slice(m * P, (m + 1) * P)
-                nc.tensor.matmul_mx(
-                    out=acc[:],
-                    lhsT=g_codes[:, toks].bitcast(E5M2X4),
-                    lhsT_scale=g_scales[:, toks],
-                    rhs=w_codes[:, cols].bitcast(E4M3X4),
-                    rhs_scale=w_scales[:, cols],
-                    start=True,
-                    stop=True,
-                )
-                nc.scalar.copy(out=stages[m][:, j * SUB : (j + 1) * SUB], in_=acc[:])
-                if j == n_sub - 1:
-                    first = (s + 1 - n_sub) * SUB
-                    nc.sync.dma_start(out=out_v[:, m, first : (s + 1) * SUB], in_=stages[m][:])
+        def multiply(s, m):
+            wc, wp = codes[s]
+            acc = psum.tile([P, SUB], F32, name="acc", tag="bank")
+            banks[(s, m)] = acc
+            toks = slice(m * P, (m + 1) * P)
+            nc.tensor.matmul_mx(
+                out=acc[:],
+                lhsT=g_codes[:, toks].bitcast(E5M2X4),
+                lhsT_scale=g_scales[:, toks],
+                rhs=wc[:].bitcast(E4M3X4),
+                rhs_scale=wp[:],
+                start=True,
+                stop=True,
+            )
 
-        prep(0)
+        def empty(s, m):
+            ends = STORE_ENDS[m]
+            end = min(e for e in ends if e > s)
+            first = max([0] + [e for e in ends if e <= s])
+            if s == first:
+                stages[m] = keep.tile([P, (end - first) * SUB], F32, name="st%d_%d" % (m, end))
+            dst = stages[m][:, (s - first) * SUB : (s - first + 1) * SUB]
+            if (s, m) in VECTOR_BANKS:
+                nc.vector.tensor_copy(out=dst, in_=banks[(s, m)][:])
+            else:
+                nc.scalar.copy(out=dst, in_=banks[(s, m)][:])
+            if s == end - 1:
+                nc.sync.dma_start(out=out_v[:, m, first * SUB : end * SUB], in_=stages[m][:])
+
+        late = []
         for s in range(N_SUB):
-            if s + 1 < N_SUB:
-                prep(s + 1)
-            quant(s)
-            multiply(s)
+            if s + 1 < N_SUB and (s + 1) not in chunk_starts:
+                regroup(s + 1, [0])
+                quantise(s)
+                regroup(s + 1, range(1, BLOCKS_PER_SUB))
+            else:
+                quantise(s)
+                if s + 1 < N_SUB:
+                    regroup(s + 1, range(BLOCKS_PER_SUB))
+            if s == N_SUB - 1:
+                for sm in late:
+                    empty(sm[0], sm[1])
+            for m in range(M_TILES):
+                multiply(s, m)
+                if (s, m) in VECTOR_BANKS and s < N_SUB - 1:
+                    late.append((s, m))
+                else:
+                    empty(s, m)

@@ -22,7 +22,7 @@ N_SUB = K // SUB
 M_TILES = TOK // P
 BLOCKS_PER_SUB = SUB // BLOCK
 
-LOAD_WIDTHS = (512, 1024, 2048, 3584)
+LOAD_WIDTHS = (1024, 2048, 4096)
 STORE_ENDS = ((3, 8, 14), (4, 9, 14), (5, 10, 14), (6, 11, 14))
 VECTOR_BANKS = ((11, 3), (12, 2), (12, 3), (13, 2), (13, 3))
 

@@ -41,7 +41,6 @@ def tile_lineardeepseekv3_kernel(tc, x, weight, weight_scale, grad_out, out):
         grp = ctx.enter_context(tc.tile_pool(name="grp", bufs=3))
         cod = ctx.enter_context(tc.tile_pool(name="cod", bufs=6))
         psum = ctx.enter_context(tc.psum_pool(name="psum", bufs=8))
-        ctx.enter_context(tc.manual_schedule())
 
         wsz = keep.tile([P, 64], BF16)
         nc.vector.memset(wsz[:], 0.0)

@@ -23,7 +23,7 @@ M_TILES = TOK // P
 BLOCKS_PER_SUB = SUB // BLOCK
 
 LOAD_WIDTHS = (1024, 2048, 4096)
-STORE_ENDS = ((3, 8, 14), (4, 9, 14), (5, 10, 14), (6, 11, 14))
+STORE_ENDS = ((2, 5, 8, 11, 14), (2, 5, 8, 11, 14), (2, 5, 8, 11, 14), (2, 5, 8, 11, 14))
 VECTOR_BANKS = ((11, 3), (12, 2), (12, 3), (13, 2), (13, 3))
 
 FLOPS = 2 * TOK * N * K
@@ -41,6 +41,7 @@ def tile_lineardeepseekv3_kernel(tc, x, weight, weight_scale, grad_out, out):
         grp = ctx.enter_context(tc.tile_pool(name="grp", bufs=3))
         cod = ctx.enter_context(tc.tile_pool(name="cod", bufs=6))
         psum = ctx.enter_context(tc.psum_pool(name="psum", bufs=8))
+        ctx.enter_context(tc.manual_schedule())
 
         wsz = keep.tile([P, 64], BF16)
         nc.vector.memset(wsz[:], 0.0)

@@ -23,7 +23,7 @@ M_TILES = TOK // P
 BLOCKS_PER_SUB = SUB // BLOCK
 
 LOAD_WIDTHS = (1024, 2048, 4096)
-STORE_ENDS = ((2, 5, 8, 11, 14), (2, 5, 8, 11, 14), (2, 5, 8, 11, 14), (2, 5, 8, 11, 14))
+STORE_ENDS = ((3, 8, 14), (4, 9, 14), (5, 10, 14), (6, 11, 14))
 VECTOR_BANKS = ((11, 3), (12, 2), (12, 3), (13, 2), (13, 3))
 
 FLOPS = 2 * TOK * N * K
@@ -44,7 +44,7 @@ def tile_lineardeepseekv3_kernel(tc, x, weight, weight_scale, grad_out, out):
         ctx.enter_context(tc.manual_schedule())
 
         wsz = keep.tile([P, 64], BF16)
-        nc.vector.memset(wsz[:], 0.0)
+        nc.gpsimd.memset(wsz[:], 0.0)
         g_sb = keep.tile([P, M_TILES * N], BF16)
         nc.sync.dma_start(out=g_sb[:], in_=g_rows.rearrange("(p m) n -> p (m n)", m=M_TILES))
         nc.sync.dma_start(out=wsz[0:P:32, 0 : K // BLOCK], in_=weight_scale)

from contextlib import ExitStack

import concourse.mybir as mybir
from concourse.masks import make_identity

F32 = mybir.dt.float32
BF16 = mybir.dt.bfloat16
U32 = mybir.dt.uint32
U8 = mybir.dt.uint8
E4M3X4 = mybir.dt.float8_e4m3fn_x4
E5M2X4 = mybir.dt.float8_e5m2_x4
MULT = mybir.AluOpType.mult

P = 128
PACK = 4
TOK = 512
N = 512
K = 7168
BLOCK = 128
SUB = 512
N_SUB = K // SUB
M_TILES = TOK // P
BLOCKS_PER_SUB = SUB // BLOCK

LOAD_WIDTHS = (1024, 2048, 4096)
STORE_ENDS = ((3, 8, 14), (4, 9, 14), (5, 10, 14), (6, 11, 14))
VECTOR_BANKS = ((11, 3), (12, 2), (12, 3), (13, 2), (13, 3))

FLOPS = 2 * TOK * N * K
BYTES = N * K * 2 + (N // BLOCK) * (K // BLOCK) * 2 + TOK * N * 2 + TOK * K * 4


def tile_lineardeepseekv3_kernel(tc, x, weight, weight_scale, grad_out, out):
    nc = tc.nc
    g_rows = grad_out.flatten_outer_dims()
    out_v = out.flatten_outer_dims().rearrange("(p m) k -> p m k", m=M_TILES)
    w_v = weight.rearrange("(p j) k -> p j k", j=PACK)

    with ExitStack() as ctx:
        keep = ctx.enter_context(tc.tile_pool(name="keep", bufs=1))
        grp = ctx.enter_context(tc.tile_pool(name="grp", bufs=3))
        cod = ctx.enter_context(tc.tile_pool(name="cod", bufs=6))
        psum = ctx.enter_context(tc.psum_pool(name="psum", bufs=8))
        ctx.enter_context(tc.manual_schedule())

        wsz = keep.tile([P, 64], BF16)
        nc.gpsimd.memset(wsz[:], 0.0)
        g_sb = keep.tile([P, M_TILES * N], BF16)
        nc.sync.dma_start(out=g_sb[:], in_=g_rows.rearrange("(p m) n -> p (m n)", m=M_TILES))
        nc.sync.dma_start(out=wsz[0:P:32, 0 : K // BLOCK], in_=weight_scale)
        raws = []
        chunk_starts = []
        c0 = 0
        for i, width in enumerate(LOAD_WIDTHS):
            raw = keep.tile([P, PACK, width], BF16, name="raw%d" % i)
            nc.sync.dma_start(out=raw[:], in_=w_v[:, :, c0 : c0 + width])
            chunk_starts.append(c0 // SUB)
            for s in range(width // SUB):
                raws.append((raw, s * SUB))
            c0 += width

        sel = keep.tile([P, P], BF16)
        nc.vector.memset(sel[:], 0.0)
        for r in range(4):
            nc.vector.memset(sel[32 * r : 32 * r + 32, 32 * r : 32 * r + 32], 1.0)
        ident = keep.tile([P, P], F32)
        make_identity(nc, ident[:])
        ws_ps = psum.tile([P, 64], F32, tag="bank")
        nc.tensor.matmul(out=ws_ps[:], lhsT=sel[:], rhs=wsz[:], start=True, stop=True)
        ws_f = keep.tile([P, 64], F32)
        nc.vector.tensor_copy(out=ws_f[:], in_=ws_ps[:])

        g_w = g_sb[:].bitcast(F32).rearrange("p (m w u) -> p m w u", m=M_TILES, u=2)
        gg = keep.tile([P, M_TILES * P * PACK], BF16, align_bytes=64)
        gg_w = gg[:].bitcast(F32).rearrange("p (m r u) -> p m r u", m=M_TILES, u=2)
        for h in range(2):
            xt = psum.tile([P, 2, 2, P], F32, tag="bank")
            for mm in range(2):
                for u in range(2):
                    nc.tensor.transpose(xt[:, mm, u, :], g_w[:, 2 * h + mm, :, u], ident[:])
            nc.scalar.copy(out=gg_w[:, 2 * h : 2 * h + 2, :, :], in_=xt[:].rearrange("p m u r -> p m r u"))

        grouped = {}
        codes = {}

        def regroup(s, blocks):
            raw, off = raws[s]
            if s not in grouped:
                grouped[s] = grp.tile([P, SUB, PACK], BF16, name="gt", align_bytes=64)
            gt = grouped[s]
            for b in blocks:
                nc.vector.tensor_scalar(
                    out=gt[:, b * BLOCK : (b + 1) * BLOCK, :].rearrange("p (c i) t -> p c t i", i=4),
                    in0=raw[:, :, off + b * BLOCK : off + (b + 1) * BLOCK].rearrange("p t (c i) -> p c t i", i=4),
                    scalar1=ws_f[:, s * BLOCKS_PER_SUB + b : s * BLOCKS_PER_SUB + b + 1],
                    scalar2=None,
                    op0=MULT,
                )

        def quantise(s):
            wc = cod.tile([P, SUB], U32, name="wc", align_bytes=64)
            wp = cod.tile([P, SUB], U8, name="wp", align_bytes=64)
            codes[s] = (wc, wp)
            nc.vector.quantize_mx(
                out=wc[:].bitcast(E4M3X4), scales=wp[:], in_=grouped[s][:].rearrange("p w t -> p (w t)")
            )

        regroup(0, range(BLOCKS_PER_SUB))
        g_codes = keep.tile([P, TOK], U32, align_bytes=64)
        g_scales = keep.tile([P, TOK], U8, align_bytes=64)
        nc.vector.quantize_mx(out=g_codes[:].bitcast(E5M2X4), scales=g_scales[:], in_=gg[:])

        stages = {}
        banks = {}

        def multiply(s, m):
            wc, wp = codes[s]
            acc = psum.tile([P, SUB], F32, name="acc", tag="bank")
            banks[(s, m)] = acc
            toks = slice(m * P, (m + 1) * P)
            nc.tensor.matmul_mx(
                out=acc[:],
                lhsT=g_codes[:, toks].bitcast(E5M2X4),
                lhsT_scale=g_scales[:, toks],
                rhs=wc[:].bitcast(E4M3X4),
                rhs_scale=wp[:],
                start=True,
                stop=True,
            )

        def empty(s, m):
            ends = STORE_ENDS[m]
            end = min(e for e in ends if e > s)
            first = max([0] + [e for e in ends if e <= s])
            if s == first:
                stages[m] = keep.tile([P, (end - first) * SUB], F32, name="st%d_%d" % (m, end))
            dst = stages[m][:, (s - first) * SUB : (s - first + 1) * SUB]
            if (s, m) in VECTOR_BANKS:
                nc.vector.tensor_copy(out=dst, in_=banks[(s, m)][:])
            else:
                nc.scalar.copy(out=dst, in_=banks[(s, m)][:])
            if s == end - 1:
                nc.sync.dma_start(out=out_v[:, m, first * SUB : end * SUB], in_=stages[m][:])

        late = []
        for s in range(N_SUB):
            if s + 1 < N_SUB and (s + 1) not in chunk_starts:
                regroup(s + 1, [0])
                quantise(s)
                regroup(s + 1, range(1, BLOCKS_PER_SUB))
            else:
                quantise(s)
                if s + 1 < N_SUB:
                    regroup(s + 1, range(BLOCKS_PER_SUB))
            if s == N_SUB - 1:
                for sm in late:
                    empty(sm[0], sm[1])
            for m in range(M_TILES):
                multiply(s, m)
                if (s, m) in VECTOR_BANKS and s < N_SUB - 1:
                    late.append((s, m))
                else:
                    empty(s, m)
